import numpy as np
import ml_dtypes


def mxq(x, axis, fmt="e4m3"):
    dtype, down = {"e4m3": (ml_dtypes.float8_e4m3fn, 7), "e5m2": (ml_dtypes.float8_e5m2, 14)}[fmt]
    v = np.moveaxis(np.asarray(x, np.float32).astype(ml_dtypes.bfloat16).astype(np.float64), axis, -1)
    blocks = v.reshape(v.shape[:-1] + (-1, 32))
    amax = np.abs(blocks).max(-1, keepdims=True)
    byte = np.maximum(np.where(amax > 0, np.frexp(amax)[1] - 1 + 127, 0) - down, 1)
    scale = np.exp2(byte - 127.0)
    codes = (blocks / scale).astype(np.float32).astype(dtype).astype(np.float64)
    return np.moveaxis((codes * scale).reshape(v.shape), -1, axis)


WIDE = False


def mx_kscale(k):
    if not WIDE:
        return np.ones(k)
    levels = np.array([10, -10, 5, -5, 0])
    a = np.random.permutation(np.resize(levels, k // 512 * 4)).reshape(k // 512, 4)
    idx = np.arange(k)
    return np.exp2(a[idx // 512, idx % 128 // 32])


BF16 = ml_dtypes.bfloat16


def bf(x):
    return np.asarray(x, np.float32).astype(BF16)


def f64(x):
    return np.asarray(x).astype(np.float64)


B, S, D, NH = 2, 64, 1024, 8
SCALE = np.sqrt(D // NH)


def setup_inputs():
    s, t = mx_kscale(D), mx_kscale(D)
    return {"x": bf(np.random.standard_normal((B, S, D)) * s),
            "wq": bf(np.random.standard_normal((D, D)) * 0.84 / np.sqrt(D) / s[None, :] * t[:, None]),
            "wk": bf(np.random.standard_normal((D, D)) * 0.84 / np.sqrt(D) / s[None, :] / t[:, None])}


def reference(x, wq, wk):
    xq = mxq(f64(x), 2, "e4m3")
    q = xq @ mxq(f64(wq), 1, "e4m3").T
    k = xq @ mxq(f64(wk), 1, "e4m3").T
    sc = (mxq(q, 2, "e4m3") @ mxq(k, 2, "e4m3").transpose(0, 2, 1)) / SCALE
    e = np.exp(sc - sc.max(-1, keepdims=True))
    return e / e.sum(-1, keepdims=True)

@@ -1,0 +1,159 @@
+from contextlib import ExitStack
+import math
+
+import concourse.masks as masks
+import concourse.mybir as mybir
+
+F32 = mybir.dt.float32
+BF16 = mybir.dt.bfloat16
+U32 = mybir.dt.uint32
+U8 = mybir.dt.uint8
+FP8X4 = mybir.dt.float8_e4m3fn_x4
+
+P = 128
+PACK = 4
+K_PASS = P * PACK
+BATCH, SEQ, D = 2, 64, 1024
+TOKENS = BATCH * SEQ
+PASSES = D // K_PASS
+WORDS = D // 2
+BLOCKS = WORDS // P
+INV_SQRT = 1.0 / math.sqrt(D // 8)
+
+FLOPS = 2 * 2 * TOKENS * D * D + 2 * BATCH * SEQ * SEQ * D
+
+
+def tile_attentionnet_pa_s_kernel(tc, x, wq, wk, out):
+    nc = tc.nc
+    weights = {"q": wq, "k": wk}
+    with ExitStack() as ctx:
+        keep = ctx.enter_context(tc.tile_pool(name="keep", bufs=1))
+        turned_pool = ctx.enter_context(tc.psum_pool(name="turned", bufs=5))
+        proj_pool = ctx.enter_context(tc.psum_pool(name="proj", bufs=2))
+        score_pool = ctx.enter_context(tc.psum_pool(name="score", bufs=1))
+        ctx.enter_context(tc.manual_schedule())
+
+        x_rows = keep.tile([P, D], BF16, name="x_rows")
+        x_grouped = keep.tile([P, D], BF16, name="x_grouped", align_bytes=64)
+        x_codes = keep.tile([P, PASSES, TOKENS], U32, name="x_codes", align_bytes=64)
+        x_scales = keep.tile([P, PASSES, TOKENS], U8, name="x_scales", align_bytes=64)
+        w_rows, w_grouped, w_codes, w_scales = {}, {}, {}, {}
+        f_grouped, f_codes, f_scales = {}, {}, {}
+        for n in weights:
+            w_rows[n] = keep.tile([P, PASSES, PACK, D], BF16, name="rows_" + n)
+            w_grouped[n] = keep.tile([P, PASSES, PACK, D], BF16, name="grouped_" + n, align_bytes=64)
+            w_codes[n] = keep.tile([P, PASSES, PACK, PASSES, P], U32, name="codes_" + n, align_bytes=64)
+            w_scales[n] = keep.tile([P, PASSES, PACK, PASSES, P], U8, name="scales_" + n, align_bytes=64)
+            f_grouped[n] = keep.tile([P, PASSES, TOKENS, PACK], BF16, name="fgrouped_" + n, align_bytes=64)
+            f_codes[n] = keep.tile([P, PASSES, TOKENS], U32, name="fcodes_" + n, align_bytes=64)
+            f_scales[n] = keep.tile([P, PASSES, TOKENS], U8, name="fscales_" + n, align_bytes=64)
+
+        nc.sync.dma_start(out=x_rows[:], in_=x.rearrange("b s d -> (b s) d"))
+        chunks = [(n, g) for g in range(PASSES) for n in ("q", "k")]
+        for n, g in chunks:
+            view = weights[n].rearrange("(g p t) d -> p g t d", g=PASSES, p=P, t=PACK)
+            for t0 in range(0, PACK, 2):
+                nc.sync.dma_start(out=w_rows[n][:, g, t0 : t0 + 2, :], in_=view[:, g, t0 : t0 + 2, :])
+
+        ident = keep.tile([P, P], F32, name="ident")
+        masks.make_identity(nc, ident[:])
+
+        zero = keep.tile([P, 1], F32, name="zero")
+        one = keep.tile([P, 1], F32, name="one")
+        nc.vector.memset(zero[:], 0.0)
+        nc.scalar.activation(out=one[:], in_=zero[:], func=mybir.ActivationFunctionType.Exp)
+
+        def turn(rows, grouped, copy):
+            turned = turned_pool.tile([P, BLOCKS, P], F32, name="turned")
+            words = rows.bitcast(F32)
+            for b in range(BLOCKS):
+                nc.tensor.transpose(turned[:, b, :], words[:, b * P : (b + 1) * P], ident[:])
+            copy(
+                out=grouped.bitcast(F32).rearrange("p (c m u) -> p c m u", c=PASSES, u=2),
+                in_=turned[:].rearrange("p (c u) m -> p c m u", u=2),
+            )
+
+        def quantise(grouped, codes, scales):
+            nc.vector.quantize_mx(out=codes.bitcast(FP8X4), scales=scales, in_=grouped)
+
+        def front(n, g):
+            for t in range(PACK):
+                copy = nc.vector.tensor_copy if t == 1 else nc.scalar.copy
+                turn(w_rows[n][:, g, t, :], w_grouped[n][:, g, t, :], copy)
+                if t > 0:
+                    quantise_rows(n, g, t - 1)
+            quantise_rows(n, g, PACK - 1)
+
+        def quantise_rows(n, g, t):
+            quantise(
+                w_grouped[n][:, g, t, :],
+                w_codes[n][:, g, t, :, :].rearrange("p c m -> p (c m)"),
+                w_scales[n][:, g, t, :, :].rearrange("p c m -> p (c m)"),
+            )
+
+        def back(n, g):
+            proj = proj_pool.tile([P, PACK, TOKENS], F32, name="proj")
+            for t in range(PACK):
+                for c in range(PASSES):
+                    nc.tensor.matmul_mx(
+                        out=proj[:, t, :],
+                        lhsT=w_codes[n][:, g, t, c, :].bitcast(FP8X4),
+                        lhsT_scale=w_scales[n][:, g, t, c, :],
+                        rhs=x_codes[:, c, :].bitcast(FP8X4),
+                        rhs_scale=x_scales[:, c, :],
+                        start=(c == 0),
+                        stop=(c == PASSES - 1),
+                    )
+            nc.scalar.copy(out=f_grouped[n][:, g, :, :], in_=proj[:].rearrange("p t n -> p n t"))
+            quantise(
+                f_grouped[n][:, g, :, :].rearrange("p n t -> p (n t)"),
+                f_codes[n][:, g, :],
+                f_scales[n][:, g, :],
+            )
+
+        turn(x_rows[:], x_grouped[:], nc.vector.tensor_copy)
+        quantise(
+            x_grouped[:],
+            x_codes[:].rearrange("p c m -> p (c m)"),
+            x_scales[:].rearrange("p c m -> p (c m)"),
+        )
+        front(*chunks[0])
+        for i in range(1, len(chunks)):
+            front(*chunks[i])
+            back(*chunks[i - 1])
+        back(*chunks[-1])
+
+        scores = score_pool.tile([P, TOKENS], F32, name="scores")
+        for g in range(PASSES):
+            nc.tensor.matmul_mx(
+                out=scores[:],
+                lhsT=f_codes["q"][:, g, :].bitcast(FP8X4),
+                lhsT_scale=f_scales["q"][:, g, :],
+                rhs=f_codes["k"][:, g, :].bitcast(FP8X4),
+                rhs_scale=f_scales["k"][:, g, :],
+                start=(g == 0),
+                stop=(g == PASSES - 1),
+            )
+
+        scaled = keep.tile([P, SEQ], F32, name="scaled")
+        nc.vector.tensor_scalar_mul(out=scaled[0:SEQ, :], in0=scores[0:SEQ, 0:SEQ], scalar1=INV_SQRT)
+        nc.scalar.mul(out=scaled[SEQ:P, :], in_=scores[SEQ:P, SEQ:P], mul=INV_SQRT)
+        neg_max = keep.tile([P, 1], F32, name="neg_max")
+        nc.vector.tensor_reduce(
+            out=neg_max[:], in_=scaled[:], axis=mybir.AxisListType.X, op=mybir.AluOpType.max, negate=True
+        )
+        expd = keep.tile([P, SEQ], F32, name="expd")
+        row_sum = keep.tile([P, 1], F32, name="row_sum")
+        nc.scalar.activation(
+            out=expd[:],
+            in_=scaled[:],
+            func=mybir.ActivationFunctionType.Exp,
+            bias=neg_max[:, 0:1],
+            scale=1.0,
+            accum_out=row_sum[:],
+        )
+        inv_sum = keep.tile([P, 1], F32, name="inv_sum")
+        nc.vector.reciprocal(out=inv_sum[:], in_=row_sum[:])
+        prob = keep.tile([P, SEQ], F32, name="prob")
+        nc.vector.tensor_scalar_mul(out=prob[:], in0=expd[:], scalar1=inv_sum[:, 0:1])
+        nc.sync.dma_start(out=out.rearrange("b s k -> (b s) k"), in_=prob[:])

@@ -19,6 +19,7 @@ PASSES = D // K_PASS
 WORDS = D // 2
 BLOCKS = WORDS // P
 INV_SQRT = 1.0 / math.sqrt(D // 8)
+WARM_PASSES = 8
 
 FLOPS = 2 * 2 * TOKENS * D * D + 2 * BATCH * SEQ * SEQ * D
 
@@ -63,6 +64,16 @@ def tile_attentionnet_pa_s_kernel(tc, x, wq, wk, out):
         nc.vector.memset(zero[:], 0.0)
         nc.scalar.activation(out=one[:], in_=zero[:], func=mybir.ActivationFunctionType.Exp)
 
+        still = keep.tile([P, P], F32, name="still")
+        nc.vector.memset(still[:], 0.0)
+        idle = score_pool.tile([P, P], F32, name="idle", tag="score")
+
+        def idle_pass():
+            nc.tensor.matmul(out=idle[:], lhsT=still[:], rhs=still[:], start=True, stop=True)
+
+        for i in range(WARM_PASSES):
+            idle_pass()
+
         def turn(rows, grouped, copy):
             turned = turned_pool.tile([P, BLOCKS, P], F32, name="turned")
             words = rows.bitcast(F32)
@@ -76,10 +87,12 @@ def tile_attentionnet_pa_s_kernel(tc, x, wq, wk, out):
         def quantise(grouped, codes, scales):
             nc.vector.quantize_mx(out=codes.bitcast(FP8X4), scales=scales, in_=grouped)
 
-        def front(n, g):
+        def front(n, g, keep_warm):
             for t in range(PACK):
                 copy = nc.vector.tensor_copy if t == 1 else nc.scalar.copy
                 turn(w_rows[n][:, g, t, :], w_grouped[n][:, g, t, :], copy)
+                if keep_warm and t % 2 == 1:
+                    idle_pass()
                 if t > 0:
                     quantise_rows(n, g, t - 1)
             quantise_rows(n, g, PACK - 1)
@@ -117,13 +130,13 @@ def tile_attentionnet_pa_s_kernel(tc, x, wq, wk, out):
             x_codes[:].rearrange("p c m -> p (c m)"),
             x_scales[:].rearrange("p c m -> p (c m)"),
         )
-        front(*chunks[0])
+        front(*chunks[0], keep_warm=True)
         for i in range(1, len(chunks)):
-            front(*chunks[i])
+            front(*chunks[i], keep_warm=(i == 1))
             back(*chunks[i - 1])
         back(*chunks[-1])
 
-        scores = score_pool.tile([P, TOKENS], F32, name="scores")
+        scores = score_pool.tile([P, TOKENS], F32, name="scores", tag="score")
         for g in range(PASSES):
             nc.tensor.matmul_mx(
                 out=scores[:],

@@ -19,7 +19,6 @@ PASSES = D // K_PASS
 WORDS = D // 2
 BLOCKS = WORDS // P
 INV_SQRT = 1.0 / math.sqrt(D // 8)
-WARM_PASSES = 8
 
 FLOPS = 2 * 2 * TOKENS * D * D + 2 * BATCH * SEQ * SEQ * D
 
@@ -51,10 +50,13 @@ def tile_attentionnet_pa_s_kernel(tc, x, wq, wk, out):
 
         nc.sync.dma_start(out=x_rows[:], in_=x.rearrange("b s d -> (b s) d"))
         chunks = [(n, g) for g in range(PASSES) for n in ("q", "k")]
-        for n, g in chunks:
+        for i, (n, g) in enumerate(chunks):
             view = weights[n].rearrange("(g p t) d -> p g t d", g=PASSES, p=P, t=PACK)
             for t0 in range(0, PACK, 2):
-                nc.sync.dma_start(out=w_rows[n][:, g, t0 : t0 + 2, :], in_=view[:, g, t0 : t0 + 2, :])
+                at_an_end = (i == 0 and t0 == 0) or (i == len(chunks) - 1 and t0 == PACK - 2)
+                step = 1 if at_an_end else 2
+                for t in range(t0, t0 + 2, step):
+                    nc.sync.dma_start(out=w_rows[n][:, g, t : t + step, :], in_=view[:, g, t : t + step, :])
 
         ident = keep.tile([P, P], F32, name="ident")
         masks.make_identity(nc, ident[:])
@@ -63,16 +65,6 @@ def tile_attentionnet_pa_s_kernel(tc, x, wq, wk, out):
         one = keep.tile([P, 1], F32, name="one")
         nc.vector.memset(zero[:], 0.0)
         nc.scalar.activation(out=one[:], in_=zero[:], func=mybir.ActivationFunctionType.Exp)
-
-        still = keep.tile([P, P], F32, name="still")
-        nc.vector.memset(still[:], 0.0)
-        idle = score_pool.tile([P, P], F32, name="idle", tag="score")
-
-        def idle_pass():
-            nc.tensor.matmul(out=idle[:], lhsT=still[:], rhs=still[:], start=True, stop=True)
-
-        for i in range(WARM_PASSES):
-            idle_pass()
 
         def turn(rows, grouped, copy):
             turned = turned_pool.tile([P, BLOCKS, P], F32, name="turned")
@@ -87,12 +79,10 @@ def tile_attentionnet_pa_s_kernel(tc, x, wq, wk, out):
         def quantise(grouped, codes, scales):
             nc.vector.quantize_mx(out=codes.bitcast(FP8X4), scales=scales, in_=grouped)
 
-        def front(n, g, keep_warm):
+        def front(n, g):
             for t in range(PACK):
                 copy = nc.vector.tensor_copy if t == 1 else nc.scalar.copy
                 turn(w_rows[n][:, g, t, :], w_grouped[n][:, g, t, :], copy)
-                if keep_warm and t % 2 == 1:
-                    idle_pass()
                 if t > 0:
                     quantise_rows(n, g, t - 1)
             quantise_rows(n, g, PACK - 1)
@@ -130,13 +120,13 @@ def tile_attentionnet_pa_s_kernel(tc, x, wq, wk, out):
             x_codes[:].rearrange("p c m -> p (c m)"),
             x_scales[:].rearrange("p c m -> p (c m)"),
         )
-        front(*chunks[0], keep_warm=True)
+        front(*chunks[0])
         for i in range(1, len(chunks)):
-            front(*chunks[i], keep_warm=(i == 1))
+            front(*chunks[i])
             back(*chunks[i - 1])
         back(*chunks[-1])
 
-        scores = score_pool.tile([P, TOKENS], F32, name="scores", tag="score")
+        scores = score_pool.tile([P, TOKENS], F32, name="scores")
         for g in range(PASSES):
             nc.tensor.matmul_mx(
                 out=scores[:],
@@ -150,7 +140,7 @@ def tile_attentionnet_pa_s_kernel(tc, x, wq, wk, out):
 
         scaled = keep.tile([P, SEQ], F32, name="scaled")
         nc.vector.tensor_scalar_mul(out=scaled[0:SEQ, :], in0=scores[0:SEQ, 0:SEQ], scalar1=INV_SQRT)
-        nc.scalar.mul(out=scaled[SEQ:P, :], in_=scores[SEQ:P, SEQ:P], mul=INV_SQRT)
+        nc.vector.tensor_scalar_mul(out=scaled[SEQ:P, :], in0=scores[SEQ:P, SEQ:P], scalar1=INV_SQRT)
         neg_max = keep.tile([P, 1], F32, name="neg_max")
         nc.vector.tensor_reduce(
             out=neg_max[:], in_=scaled[:], axis=mybir.AxisListType.X, op=mybir.AluOpType.max, negate=True

from contextlib import ExitStack
import math

import concourse.masks as masks
import concourse.mybir as mybir

F32 = mybir.dt.float32
BF16 = mybir.dt.bfloat16
U32 = mybir.dt.uint32
U8 = mybir.dt.uint8
FP8X4 = mybir.dt.float8_e4m3fn_x4

P = 128
PACK = 4
K_PASS = P * PACK
BATCH, SEQ, D = 2, 64, 1024
TOKENS = BATCH * SEQ
PASSES = D // K_PASS
WORDS = D // 2
BLOCKS = WORDS // P
INV_SQRT = 1.0 / math.sqrt(D // 8)

FLOPS = 2 * 2 * TOKENS * D * D + 2 * BATCH * SEQ * SEQ * D


def tile_attentionnet_pa_s_kernel(tc, x, wq, wk, out):
    nc = tc.nc
    weights = {"q": wq, "k": wk}
    with ExitStack() as ctx:
        keep = ctx.enter_context(tc.tile_pool(name="keep", bufs=1))
        turned_pool = ctx.enter_context(tc.psum_pool(name="turned", bufs=5))
        proj_pool = ctx.enter_context(tc.psum_pool(name="proj", bufs=2))
        score_pool = ctx.enter_context(tc.psum_pool(name="score", bufs=1))
        ctx.enter_context(tc.manual_schedule())

        x_rows = keep.tile([P, D], BF16, name="x_rows")
        x_grouped = keep.tile([P, D], BF16, name="x_grouped", align_bytes=64)
        x_codes = keep.tile([P, PASSES, TOKENS], U32, name="x_codes", align_bytes=64)
        x_scales = keep.tile([P, PASSES, TOKENS], U8, name="x_scales", align_bytes=64)
        w_rows, w_grouped, w_codes, w_scales = {}, {}, {}, {}
        f_grouped, f_codes, f_scales = {}, {}, {}
        for n in weights:
            w_rows[n] = keep.tile([P, PASSES, PACK, D], BF16, name="rows_" + n)
            w_grouped[n] = keep.tile([P, PASSES, PACK, D], BF16, name="grouped_" + n, align_bytes=64)
            w_codes[n] = keep.tile([P, PASSES, PACK, PASSES, P], U32, name="codes_" + n, align_bytes=64)
            w_scales[n] = keep.tile([P, PASSES, PACK, PASSES, P], U8, name="scales_" + n, align_bytes=64)
            f_grouped[n] = keep.tile([P, PASSES, TOKENS, PACK], BF16, name="fgrouped_" + n, align_bytes=64)
            f_codes[n] = keep.tile([P, PASSES, TOKENS], U32, name="fcodes_" + n, align_bytes=64)
            f_scales[n] = keep.tile([P, PASSES, TOKENS], U8, name="fscales_" + n, align_bytes=64)

        nc.sync.dma_start(out=x_rows[:], in_=x.rearrange("b s d -> (b s) d"))
        chunks = [(n, g) for g in range(PASSES) for n in ("q", "k")]
        for i, (n, g) in enumerate(chunks):
            view = weights[n].rearrange("(g p t) d -> p g t d", g=PASSES, p=P, t=PACK)
            for t0 in range(0, PACK, 2):
                at_an_end = (i == 0 and t0 == 0) or (i == len(chunks) - 1 and t0 == PACK - 2)
                step = 1 if at_an_end else 2
                for t in range(t0, t0 + 2, step):
                    nc.sync.dma_start(out=w_rows[n][:, g, t : t + step, :], in_=view[:, g, t : t + step, :])

        ident = keep.tile([P, P], F32, name="ident")
        masks.make_identity(nc, ident[:])

        zero = keep.tile([P, 1], F32, name="zero")
        one = keep.tile([P, 1], F32, name="one")
        nc.vector.memset(zero[:], 0.0)
        nc.scalar.activation(out=one[:], in_=zero[:], func=mybir.ActivationFunctionType.Exp)

        def turn(rows, grouped, copy):
            turned = turned_pool.tile([P, BLOCKS, P], F32, name="turned")
            words = rows.bitcast(F32)
            for b in range(BLOCKS):
                nc.tensor.transpose(turned[:, b, :], words[:, b * P : (b + 1) * P], ident[:])
            copy(
                out=grouped.bitcast(F32).rearrange("p (c m u) -> p c m u", c=PASSES, u=2),
                in_=turned[:].rearrange("p (c u) m -> p c m u", u=2),
            )

        def quantise(grouped, codes, scales):
            nc.vector.quantize_mx(out=codes.bitcast(FP8X4), scales=scales, in_=grouped)

        def front(n, g):
            for t in range(PACK):
                copy = nc.vector.tensor_copy if t == 1 else nc.scalar.copy
                turn(w_rows[n][:, g, t, :], w_grouped[n][:, g, t, :], copy)
                if t > 0:
                    quantise_rows(n, g, t - 1)
            quantise_rows(n, g, PACK - 1)

        def quantise_rows(n, g, t):
            quantise(
                w_grouped[n][:, g, t, :],
                w_codes[n][:, g, t, :, :].rearrange("p c m -> p (c m)"),
                w_scales[n][:, g, t, :, :].rearrange("p c m -> p (c m)"),
            )

        def back(n, g):
            proj = proj_pool.tile([P, PACK, TOKENS], F32, name="proj")
            for t in range(PACK):
                for c in range(PASSES):
                    nc.tensor.matmul_mx(
                        out=proj[:, t, :],
                        lhsT=w_codes[n][:, g, t, c, :].bitcast(FP8X4),
                        lhsT_scale=w_scales[n][:, g, t, c, :],
                        rhs=x_codes[:, c, :].bitcast(FP8X4),
                        rhs_scale=x_scales[:, c, :],
                        start=(c == 0),
                        stop=(c == PASSES - 1),
                    )
            nc.scalar.copy(out=f_grouped[n][:, g, :, :], in_=proj[:].rearrange("p t n -> p n t"))
            quantise(
                f_grouped[n][:, g, :, :].rearrange("p n t -> p (n t)"),
                f_codes[n][:, g, :],
                f_scales[n][:, g, :],
            )

        turn(x_rows[:], x_grouped[:], nc.vector.tensor_copy)
        quantise(
            x_grouped[:],
            x_codes[:].rearrange("p c m -> p (c m)"),
            x_scales[:].rearrange("p c m -> p (c m)"),
        )
        front(*chunks[0])
        for i in range(1, len(chunks)):
            front(*chunks[i])
            back(*chunks[i - 1])
        back(*chunks[-1])

        scores = score_pool.tile([P, TOKENS], F32, name="scores")
        for g in range(PASSES):
            nc.tensor.matmul_mx(
                out=scores[:],
                lhsT=f_codes["q"][:, g, :].bitcast(FP8X4),
                lhsT_scale=f_scales["q"][:, g, :],
                rhs=f_codes["k"][:, g, :].bitcast(FP8X4),
                rhs_scale=f_scales["k"][:, g, :],
                start=(g == 0),
                stop=(g == PASSES - 1),
            )

        scaled = keep.tile([P, SEQ], F32, name="scaled")
        nc.vector.tensor_scalar_mul(out=scaled[0:SEQ, :], in0=scores[0:SEQ, 0:SEQ], scalar1=INV_SQRT)
        nc.vector.tensor_scalar_mul(out=scaled[SEQ:P, :], in0=scores[SEQ:P, SEQ:P], scalar1=INV_SQRT)
        neg_max = keep.tile([P, 1], F32, name="neg_max")
        nc.vector.tensor_reduce(
            out=neg_max[:], in_=scaled[:], axis=mybir.AxisListType.X, op=mybir.AluOpType.max, negate=True
        )
        expd = keep.tile([P, SEQ], F32, name="expd")
        row_sum = keep.tile([P, 1], F32, name="row_sum")
        nc.scalar.activation(
            out=expd[:],
            in_=scaled[:],
            func=mybir.ActivationFunctionType.Exp,
            bias=neg_max[:, 0:1],
            scale=1.0,
            accum_out=row_sum[:],
        )
        inv_sum = keep.tile([P, 1], F32, name="inv_sum")
        nc.vector.reciprocal(out=inv_sum[:], in_=row_sum[:])
        prob = keep.tile([P, SEQ], F32, name="prob")
        nc.vector.tensor_scalar_mul(out=prob[:], in0=expd[:], scalar1=inv_sum[:, 0:1])
        nc.sync.dma_start(out=out.rearrange("b s k -> (b s) k"), in_=prob[:])
